import numpy as np
import ml_dtypes


def mxq(x, axis, fmt="e4m3"):
    dtype, down = {"e4m3": (ml_dtypes.float8_e4m3fn, 7), "e5m2": (ml_dtypes.float8_e5m2, 14)}[fmt]
    v = np.moveaxis(np.asarray(x, np.float32).astype(ml_dtypes.bfloat16).astype(np.float64), axis, -1)
    blocks = v.reshape(v.shape[:-1] + (-1, 32))
    amax = np.abs(blocks).max(-1, keepdims=True)
    byte = np.maximum(np.where(amax > 0, np.frexp(amax)[1] - 1 + 127, 0) - down, 1)
    scale = np.exp2(byte - 127.0)
    codes = (blocks / scale).astype(np.float32).astype(dtype).astype(np.float64)
    return np.moveaxis((codes * scale).reshape(v.shape), -1, axis)


WIDE = False


def mx_kscale(k):
    if not WIDE:
        return np.ones(k)
    levels = np.array([10, -10, 5, -5, 0])
    a = np.random.permutation(np.resize(levels, k // 512 * 4)).reshape(k // 512, 4)
    idx = np.arange(k)
    return np.exp2(a[idx // 512, idx % 128 // 32])


BF16 = ml_dtypes.bfloat16


def bf(x):
    return np.asarray(x, np.float32).astype(BF16)


def f64(x):
    return np.asarray(x).astype(np.float64)


E2M1 = np.array([0.0, 0.5, 1.0, 1.5, 2.0, 3.0, 4.0, 6.0, -0.0, -0.5, -1.0, -1.5, -2.0, -3.0, -4.0, -6.0])


def pack_weight(w, fmt):
    k, n = w.shape
    w = f64(bf(w)).reshape(k // 32, 32, n)
    amax = np.abs(w).max(1)
    if fmt == "e4m3":
        byte = np.frexp(amax)[1] - 1 + 127 - 7
    else:
        mant, ex = np.frexp(amax / 6.0)
        byte = np.where(mant > 0.5, ex, ex - 1) + 127
    byte = np.clip(np.where(amax > 0, byte, 1), 1, 254)
    scaled = (w * np.exp2(127.0 - byte)[:, None, :]).reshape(k, n).astype(np.float32)
    by_word = np.ascontiguousarray(scaled.reshape(k // 512, 128, 4, n).transpose(0, 1, 3, 2))
    if fmt == "e4m3":
        words = by_word.astype(ml_dtypes.float8_e4m3fn).view(np.uint8)
    else:
        c = by_word.astype(ml_dtypes.float4_e2m1fn).view(np.uint8) & 0xF
        words = c[..., 0::2] | (c[..., 1::2] << 4)
    return np.ascontiguousarray(words), np.ascontiguousarray(byte.astype(np.uint8).reshape(k // 512, 16, n))


def unpack_weight(words, scales, fmt):
    g, p, n, _ = words.shape
    if fmt == "e4m3":
        vals = np.ascontiguousarray(words).view(ml_dtypes.float8_e4m3fn).astype(np.float64)
    else:
        nib = np.empty((g, p, n, 4), np.uint8)
        nib[..., 0::2] = words & 0xF
        nib[..., 1::2] = words >> 4
        vals = E2M1[nib]
    vals = vals * np.repeat(np.exp2(scales.astype(np.float64) - 127.0), 8, axis=1)[..., None]
    return vals.transpose(0, 1, 3, 2).reshape(g * 512, n)

def pack4(w):
    words, scales = pack_weight(w, "e2m1")
    return words.reshape(words.shape[0], 128, -1), scales


def unpack4(words, scales):
    return unpack_weight(words.reshape(words.shape[0], 128, -1, 2), scales, "e2m1")


B, N, DIM, R, KEY = 1, 1024, 1024, 4, 128
UV = DIM * R // 2
WI = DIM * R + KEY


def silu(z):
    return z / (1.0 + np.exp(-z))


def rope_tables(n, d):
    half = d // 2
    omega = 1.0 / (10000.0 ** (np.arange(half) / half))
    ang = np.arange(n)[:, None] * omega[None, :]
    return np.sin(ang), np.cos(ang)


def apply_rotary(x, sin, cos):
    x1, x2 = x[..., 0::2], x[..., 1::2]
    return np.concatenate([x1 * cos - x2 * sin, x1 * sin + x2 * cos], axis=-1)


def setup_inputs():
    s = mx_kscale(DIM)
    hidden_states = bf(np.random.standard_normal((B, N, DIM)) * s)
    Wi_words, Wi_scales = pack4(np.random.standard_normal((DIM, WI)) / np.sqrt(DIM) / s[:, None])
    return {"hidden_states": hidden_states,
            "Wi_words": Wi_words,
            "Wi_scales": Wi_scales,
            "bi": bf(np.random.standard_normal(WI) * 0.1),
            "q_gamma": bf(2.0 + 0.2 * np.random.standard_normal(KEY)),
            "q_beta": bf(0.3 * np.random.standard_normal(KEY)),
            "k_gamma": bf(2.0 + 0.2 * np.random.standard_normal(KEY)),
            "k_beta": bf(0.3 * np.random.standard_normal(KEY))}


def reference(hidden_states, Wi_words, Wi_scales, bi, q_gamma, q_beta, k_gamma, k_beta):
    sin, cos = rope_tables(N, KEY)
    x = silu((mxq(f64(hidden_states), 2, "e4m3") @ unpack4(Wi_words, Wi_scales)) + f64(bi))
    u = x[..., :UV]
    v = x[..., UV:2 * UV]
    qk = x[..., 2 * UV:]
    q = apply_rotary(qk * f64(q_gamma) + f64(q_beta), sin, cos)
    k = apply_rotary(qk * f64(k_gamma) + f64(k_beta), sin, cos)
    return u, v, q, k

@@ -1,0 +1,278 @@
+import math
+from contextlib import ExitStack
+
+import concourse.mybir as mybir
+from concourse.masks import make_identity
+
+F32 = mybir.dt.float32
+BF16 = mybir.dt.bfloat16
+I32 = mybir.dt.int32
+U32 = mybir.dt.uint32
+U8 = mybir.dt.uint8
+FP8X4 = mybir.dt.float8_e4m3fn_x4
+FP4X4 = mybir.dt.float4_e2m1fn_x4
+ALU = mybir.AluOpType
+ACT = mybir.ActivationFunctionType
+
+P = 128
+TOKENS = 1024
+DIM = 1024
+UV = 2048
+KEY = 128
+HALF = KEY // 2
+WI = 2 * UV + KEY
+TILES = TOKENS // P
+K_PASS = 4 * P
+PASSES = DIM // K_PASS
+BANK = 512
+W_CHUNK = 1024
+ROUND_MAGIC = 1.5 * 2.0**23
+
+FLOPS = 2 * TOKENS * DIM * WI
+
+
+def tile_gau_ae_pa_kernel(
+    tc, hidden_states, Wi_words, Wi_scales, bi, q_gamma, q_beta, k_gamma, k_beta, out_0, out_1, out_2, out_3
+):
+    nc = tc.nc
+    x_dram = hidden_states.flatten_outer_dims().rearrange("(p t) k -> p t k", t=TILES)
+    uv_dram = [o.flatten_outer_dims().rearrange("(p t) n -> p t n", t=TILES) for o in (out_0, out_1)]
+    qk_dram = [o.flatten_outer_dims().rearrange("(p t) f -> p t f", t=TILES) for o in (out_2, out_3)]
+
+    with ExitStack() as ctx:
+        keep = ctx.enter_context(tc.tile_pool(name="keep", bufs=1))
+        stage = ctx.enter_context(tc.tile_pool(name="stage", bufs=4))
+        zpool = ctx.enter_context(tc.tile_pool(name="zpool", bufs=6))
+        qkpool = ctx.enter_context(tc.tile_pool(name="qkpool", bufs=3))
+        psum = ctx.enter_context(tc.psum_pool(name="psum", bufs=8))
+
+        ctx.enter_context(tc.manual_schedule())
+
+        ident_f32 = keep.tile([P, P], F32)
+        make_identity(nc, ident_f32[:])
+        position_i = keep.tile([P, TILES], I32)
+        nc.gpsimd.iota(position_i[:], pattern=[[1, TILES]], base=0, channel_multiplier=TILES)
+
+        bias_rows = keep.tile([P, BANK], BF16)
+        small_rows = keep.tile([P, BANK], BF16)
+        nc.vector.memset(bias_rows[:].bitcast(I32), 0)
+        nc.vector.memset(small_rows[:].bitcast(I32), 0)
+        nc.scalar.dma_start(out=bias_rows[0:8, :], in_=bi[0 : 2 * UV].rearrange("(c n) -> c n", n=BANK))
+
+        warm = keep.tile([P, 1], F32)
+        nc.vector.memset(warm[:], 0.0)
+        nc.scalar.activation(out=warm[:], in_=warm[:], func=ACT.Silu)
+
+        x_raw = keep.tile([P, TILES, DIM], BF16)
+
+        def load_tokens(t):
+            nc.sync.dma_start(out=x_raw[:, t : t + 2, :], in_=x_dram[:, t : t + 2, :])
+
+        w_dram = Wi_words.rearrange("g p b -> p g b")
+        w_words = {}
+
+        def load_weights(chunk):
+            first, last = W_CHUNK * chunk, min(W_CHUNK * (chunk + 1), WI)
+            w_words[chunk] = keep.tile([P, PASSES, 2 * (last - first)], U8, align_bytes=64, name="w_words_%d" % chunk)
+            nc.sync.dma_start(
+                out=w_words[chunk][:].bitcast(I32), in_=w_dram[:, :, 2 * first : 2 * last].bitcast(I32)
+            )
+
+        load_tokens(0)
+
+        w_scales = keep.tile([P, PASSES, WI], U8, align_bytes=64)
+        nc.vector.memset(w_scales[:].bitcast(I32), 0)
+        for r in range(4):
+            nc.sync.dma_start(
+                out=w_scales[r:P:32, :, :].bitcast(I32),
+                in_=Wi_scales[:, r:16:4, :].rearrange("g q n -> q g n").bitcast(I32),
+            )
+
+        load_weights(0)
+        load_weights(1)
+        load_tokens(2)
+        load_weights(2)
+        load_weights(3)
+        load_weights(4)
+        for v, vector in enumerate((bi[2 * UV : WI], q_gamma, k_gamma, q_beta, k_beta)):
+            row, slot = v // 4, v % 4
+            nc.sync.dma_start(
+                out=small_rows[row : row + 1, KEY * slot : KEY * (slot + 1)],
+                in_=vector.rearrange("(o n) -> o n", o=1),
+            )
+        load_tokens(4)
+        load_tokens(6)
+
+        ident_bf16 = keep.tile([P, P], BF16)
+        nc.vector.tensor_copy(out=ident_bf16[:], in_=ident_f32[:])
+        per_turn = keep.tile([P, HALF], F32)
+        nc.vector.memset(per_turn[:, 0:1], 1.0)
+        nc.vector.tensor_scalar_mul(out=per_turn[:, 0:1], in0=per_turn[:, 0:1], scalar1=1.0 / (2.0 * math.pi))
+        for w in (1, 2, 4, 8, 16, 32):
+            nc.vector.tensor_scalar_mul(
+                out=per_turn[:, w : 2 * w], in0=per_turn[:, 0:w], scalar1=10000.0 ** (-w / HALF)
+            )
+        position = keep.tile([P, TILES], F32)
+        nc.vector.tensor_copy(out=position[:], in_=position_i[:])
+        turns = keep.tile([P, 2, TILES, HALF], F32)
+        nc.vector.tensor_tensor(
+            out=turns[:, 1, :, :],
+            in0=per_turn[:].unsqueeze(1).to_broadcast([P, TILES, HALF]),
+            in1=position[:].unsqueeze(2).to_broadcast([P, TILES, HALF]),
+            op=ALU.mult,
+        )
+        nc.vector.tensor_scalar_add(out=turns[:, 0, :, :], in0=turns[:, 1, :, :], scalar1=0.25)
+        whole = keep.tile([P, 2, TILES, HALF], F32)
+        nc.vector.tensor_scalar(
+            out=whole[:], in0=turns[:], scalar1=ROUND_MAGIC, scalar2=ROUND_MAGIC, op0=ALU.add, op1=ALU.subtract
+        )
+        nc.vector.tensor_tensor(out=turns[:], in0=turns[:], in1=whole[:], op=ALU.subtract)
+
+        spread = keep.tile([P, 10 * BANK], BF16)
+
+        def spread_rows(source, row, pair):
+            copies = psum.tile([P, 2 * BANK], BF16, tag="bank")
+            for i in range(2):
+                nc.tensor.matmul(
+                    copies[:, BANK * i : BANK * (i + 1)],
+                    lhsT=ident_bf16[:, row + i : row + i + 1].to_broadcast([P, P]),
+                    rhs=source[:],
+                    start=True,
+                    stop=True,
+                )
+            nc.scalar.copy(out=spread[:, 2 * BANK * pair : 2 * BANK * (pair + 1)], in_=copies[:])
+
+        x_words = x_raw[:].bitcast(F32)
+        x_codes = keep.tile([P, TILES, PASSES * P], U32, align_bytes=64)
+        x_scales = keep.tile([P, TILES, PASSES * P], U8, align_bytes=64)
+
+        def flip(t):
+            flipped = psum.tile([P, PASSES, 2, P], F32, tag="bank")
+            for g in range(PASSES):
+                for u in range(2):
+                    nc.tensor.transpose(
+                        flipped[:, g, u, :], x_words[:, t, 256 * g + u : 256 * (g + 1) : 2], ident_f32[:]
+                    )
+            grouped = stage.tile([P, PASSES, P, 4], BF16, align_bytes=64, tag="grouped")
+            nc.scalar.copy(out=grouped[:].bitcast(F32), in_=flipped[:].rearrange("p g u r -> p g r u"))
+            return grouped
+
+        def quantise(t, grouped):
+            nc.vector.quantize_mx(
+                out=x_codes[:, t, :].bitcast(FP8X4),
+                scales=x_scales[:, t, :],
+                in_=grouped[:].rearrange("p g r j -> p (g r j)"),
+            )
+
+        spread_rows(bias_rows, 0, 0)
+        ahead = [flip(0), flip(1)]
+        quantise(0, ahead[0])
+        quantise(1, ahead[1])
+        for pair in range(1, 4):
+            spread_rows(bias_rows, 2 * pair, pair)
+
+        cos_sin = keep.tile([P, 2, TILES, HALF], F32)
+        nc.scalar.activation(out=cos_sin[:], in_=turns[:], func=ACT.Sin, scale=2.0 * math.pi)
+
+
+        def project(t, acc, first, width):
+            chunk, inside = first // W_CHUNK, first % W_CHUNK
+            for g in range(PASSES):
+                nc.tensor.matmul_mx(
+                    out=acc,
+                    lhsT=x_codes[:, t, P * g : P * (g + 1)].bitcast(FP8X4),
+                    lhsT_scale=x_scales[:, t, P * g : P * (g + 1)],
+                    rhs=w_words[chunk][:, g, 2 * inside : 2 * (inside + width)].bitcast(FP4X4),
+                    rhs_scale=w_scales[:, g, first : first + width],
+                    start=(g == 0),
+                    stop=(g == PASSES - 1),
+                )
+
+        halves = keep.tile([P, 5, KEY], F32)
+
+        def q_and_k(first, count):
+            acc_qk = psum.tile([P, count, KEY], F32, tag="bank")
+            for i in range(count):
+                project(first + i, acc_qk[:, i, :], 2 * UV, KEY)
+            qk = qkpool.tile([P, count, KEY], F32, tag="qk")
+            nc.vector.tensor_tensor(
+                out=qk[:].rearrange("p t (h j) -> p t h j", h=2),
+                in0=acc_qk[:].rearrange("p t (j h) -> p t h j", h=2),
+                in1=halves[:, 0:1, :].to_broadcast([P, count, KEY]).rearrange("p t (h j) -> p t h j", h=2),
+                op=ALU.add,
+            )
+            nc.scalar.activation(out=qk[:], in_=qk[:], func=ACT.Silu)
+            scaled = qkpool.tile([P, count, 2, KEY], F32, tag="scaled")
+            nc.gpsimd.tensor_tensor(
+                out=scaled[:],
+                in0=qk[:].unsqueeze(2).to_broadcast([P, count, 2, KEY]),
+                in1=halves[:, 1:3, :].unsqueeze(1).to_broadcast([P, count, 2, KEY]),
+                op=ALU.mult,
+            )
+            nc.gpsimd.tensor_tensor(
+                out=scaled[:],
+                in0=scaled[:],
+                in1=halves[:, 3:5, :].unsqueeze(1).to_broadcast([P, count, 2, KEY]),
+                op=ALU.add,
+            )
+            x1, x2 = scaled[:, :, :, 0:HALF], scaled[:, :, :, HALF:KEY]
+            cos = cos_sin[:, 0, first : first + count, :].unsqueeze(2).to_broadcast([P, count, 2, HALF])
+            sin = cos_sin[:, 1, first : first + count, :].unsqueeze(2).to_broadcast([P, count, 2, HALF])
+            rotated = qkpool.tile([P, 2, count, KEY], F32, tag="rotated")
+            by_token = rotated[:].rearrange("p c t f -> p t c f")
+            for out, with_x1, with_x2, op in (
+                (by_token[:, :, :, 0:HALF], cos, sin, ALU.subtract),
+                (by_token[:, :, :, HALF:KEY], sin, cos, ALU.add),
+            ):
+                left = qkpool.tile([P, count, 2, HALF], F32, tag="left")
+                right = qkpool.tile([P, count, 2, HALF], F32, tag="right")
+                nc.gpsimd.tensor_tensor(out=left[:], in0=x1, in1=with_x1, op=ALU.mult)
+                nc.gpsimd.tensor_tensor(out=right[:], in0=x2, in1=with_x2, op=ALU.mult)
+                nc.gpsimd.tensor_tensor(out=out, in0=left[:], in1=right[:], op=op)
+            return first, count, rotated
+
+        def silu_and_store(t, half, first_bank, banks):
+            z = zpool.tile([P, BANK * banks], F32, tag="z%d" % banks)
+            for b in range(banks):
+                first = UV * half + BANK * (first_bank + b)
+                acc = psum.tile([P, BANK], F32, tag="bank")
+                project(t, acc[:], first, BANK)
+                nc.vector.tensor_tensor(
+                    out=z[:, BANK * b : BANK * (b + 1)], in0=acc[:], in1=spread[:, first : first + BANK], op=ALU.add
+                )
+            nc.scalar.activation(out=z[:], in_=z[:], func=ACT.Silu)
+            nc.sync.dma_start(
+                out=uv_dram[half][:, t, BANK * first_bank : BANK * (first_bank + banks)], in_=z[:]
+            )
+
+        banks_of_half = UV // BANK
+        in_work = []
+        for t in range(0, TILES, 2):
+            more = t + 2 < TILES
+            silu_and_store(t, 0, 0, banks_of_half)
+            if more:
+                ahead = [flip(t + 2), flip(t + 3)]
+            silu_and_store(t + 1, 0, 0, banks_of_half)
+            if t == 0:
+                spread_rows(small_rows, 0, 4)
+            silu_and_store(t, 1, 0, banks_of_half)
+            if more:
+                quantise(t + 2, ahead[0])
+                quantise(t + 3, ahead[1])
+            if t == 0:
+                nc.vector.tensor_copy(
+                    out=halves[:].rearrange("p v (h j) -> p v h j", h=2),
+                    in_=spread[:, 2 * UV : 2 * UV + 5 * KEY].rearrange("p (v j h) -> p v h j", v=5, h=2),
+                )
+                first_batch = q_and_k(0, 2)
+            if more:
+                silu_and_store(t + 1, 1, 0, banks_of_half)
+            else:
+                for b in range(banks_of_half):
+                    silu_and_store(t + 1, 1, b, 1)
+            for first, count, rotated in in_work:
+                for c in range(2):
+                    nc.sync.dma_start(out=qk_dram[c][:, first : first + count, :], in_=rotated[:, c, :, :])
+            in_work = [first_batch] if t == 0 else []
+            if more:
+                in_work.append(q_and_k(t + 2, 2))

@@ -26,6 +26,8 @@ K_PASS = 4 * P
 PASSES = DIM // K_PASS
 BANK = 512
 W_CHUNK = 1024
+SCALE_SPLIT = UV
+WARM_UP = 4
 ROUND_MAGIC = 1.5 * 2.0**23
 
 FLOPS = 2 * TOKENS * DIM * WI
@@ -53,20 +55,35 @@ def tile_gau_ae_pa_kernel(
         position_i = keep.tile([P, TILES], I32)
         nc.gpsimd.iota(position_i[:], pattern=[[1, TILES]], base=0, channel_multiplier=TILES)
 
+        scale_tiles = []
+        for i, (first, last) in enumerate(((0, SCALE_SPLIT), (SCALE_SPLIT, WI))):
+            plane = keep.tile([P, PASSES, last - first], U8, align_bytes=64, name="w_scales_%d" % i)
+            scale_tiles.append((first, last, plane))
         bias_rows = keep.tile([P, BANK], BF16)
         small_rows = keep.tile([P, BANK], BF16)
+        warm = keep.tile([P, 1], F32)
+        zeros = keep.tile([P, BANK], BF16)
+        nc.vector.memset(warm[:], 0.0)
         nc.vector.memset(bias_rows[:].bitcast(I32), 0)
+        nc.vector.memset(zeros[:].bitcast(I32), 0)
+        nc.vector.memset(scale_tiles[0][2][:].bitcast(I32), 0)
         nc.vector.memset(small_rows[:].bitcast(I32), 0)
+        nc.vector.memset(scale_tiles[1][2][:].bitcast(I32), 0)
         nc.scalar.dma_start(out=bias_rows[0:8, :], in_=bi[0 : 2 * UV].rearrange("(c n) -> c n", n=BANK))
 
-        warm = keep.tile([P, 1], F32)
-        nc.vector.memset(warm[:], 0.0)
         nc.scalar.activation(out=warm[:], in_=warm[:], func=ACT.Silu)
 
-        x_raw = keep.tile([P, TILES, DIM], BF16)
+        idle = psum.tile([P, BANK], F32, tag="bank")
+        for i in range(WARM_UP):
+            nc.tensor.matmul(idle[:], lhsT=zeros[:, 0:P], rhs=zeros[:], start=True, stop=True)
 
-        def load_tokens(t):
-            nc.sync.dma_start(out=x_raw[:, t : t + 2, :], in_=x_dram[:, t : t + 2, :])
+        x_words = {}
+
+        def load_tokens(t, count):
+            x_raw = keep.tile([P, count, DIM], BF16, name="x_raw_%d" % t)
+            nc.sync.dma_start(out=x_raw[:], in_=x_dram[:, t : t + count, :])
+            for i in range(count):
+                x_words[t + i] = x_raw[:, i, :].bitcast(F32)
 
         w_dram = Wi_words.rearrange("g p b -> p g b")
         w_words = {}
@@ -78,21 +95,24 @@ def tile_gau_ae_pa_kernel(
                 out=w_words[chunk][:].bitcast(I32), in_=w_dram[:, :, 2 * first : 2 * last].bitcast(I32)
             )
 
-        load_tokens(0)
+        def load_scales(i):
+            first, last, plane = scale_tiles[i]
+            for r in range(4):
+                nc.sync.dma_start(
+                    out=plane[r:P:32, :, :].bitcast(I32),
+                    in_=Wi_scales[:, r:16:4, first:last].rearrange("g q n -> q g n").bitcast(I32),
+                )
 
-        w_scales = keep.tile([P, PASSES, WI], U8, align_bytes=64)
-        nc.vector.memset(w_scales[:].bitcast(I32), 0)
-        for r in range(4):
-            nc.sync.dma_start(
-                out=w_scales[r:P:32, :, :].bitcast(I32),
-                in_=Wi_scales[:, r:16:4, :].rearrange("g q n -> q g n").bitcast(I32),
-            )
-
+        load_tokens(0, 1)
+        load_scales(0)
         load_weights(0)
+        load_tokens(1, 1)
         load_weights(1)
-        load_tokens(2)
+        load_tokens(2, 2)
+        load_scales(1)
         load_weights(2)
         load_weights(3)
+        load_tokens(4, 2)
         load_weights(4)
         for v, vector in enumerate((bi[2 * UV : WI], q_gamma, k_gamma, q_beta, k_beta)):
             row, slot = v // 4, v % 4
@@ -100,90 +120,93 @@ def tile_gau_ae_pa_kernel(
                 out=small_rows[row : row + 1, KEY * slot : KEY * (slot + 1)],
                 in_=vector.rearrange("(o n) -> o n", o=1),
             )
-        load_tokens(4)
-        load_tokens(6)
+        load_tokens(6, 2)
 
         ident_bf16 = keep.tile([P, P], BF16)
         nc.vector.tensor_copy(out=ident_bf16[:], in_=ident_f32[:])
-        per_turn = keep.tile([P, HALF], F32)
-        nc.vector.memset(per_turn[:, 0:1], 1.0)
-        nc.vector.tensor_scalar_mul(out=per_turn[:, 0:1], in0=per_turn[:, 0:1], scalar1=1.0 / (2.0 * math.pi))
-        for w in (1, 2, 4, 8, 16, 32):
-            nc.vector.tensor_scalar_mul(
-                out=per_turn[:, w : 2 * w], in0=per_turn[:, 0:w], scalar1=10000.0 ** (-w / HALF)
-            )
         position = keep.tile([P, TILES], F32)
         nc.vector.tensor_copy(out=position[:], in_=position_i[:])
+        per_turn = keep.tile([P, HALF], F32)
+        nc.gpsimd.memset(per_turn[:, 0:1], 1.0)
+        nc.gpsimd.tensor_scalar(
+            out=per_turn[:, 0:1], in0=per_turn[:, 0:1], scalar1=1.0 / (2.0 * math.pi), scalar2=0.0,
+            op0=ALU.mult, op1=ALU.add,
+        )
+        for w in (1, 2, 4, 8, 16, 32):
+            nc.gpsimd.tensor_scalar(
+                out=per_turn[:, w : 2 * w], in0=per_turn[:, 0:w], scalar1=10000.0 ** (-w / HALF), scalar2=0.0,
+                op0=ALU.mult, op1=ALU.add,
+            )
         turns = keep.tile([P, 2, TILES, HALF], F32)
-        nc.vector.tensor_tensor(
+        nc.gpsimd.tensor_tensor(
             out=turns[:, 1, :, :],
             in0=per_turn[:].unsqueeze(1).to_broadcast([P, TILES, HALF]),
             in1=position[:].unsqueeze(2).to_broadcast([P, TILES, HALF]),
             op=ALU.mult,
         )
-        nc.vector.tensor_scalar_add(out=turns[:, 0, :, :], in0=turns[:, 1, :, :], scalar1=0.25)
+        nc.gpsimd.tensor_scalar(
+            out=turns[:, 0, :, :], in0=turns[:, 1, :, :], scalar1=0.25, scalar2=0.0, op0=ALU.add, op1=ALU.add
+        )
         whole = keep.tile([P, 2, TILES, HALF], F32)
-        nc.vector.tensor_scalar(
+        nc.gpsimd.tensor_scalar(
             out=whole[:], in0=turns[:], scalar1=ROUND_MAGIC, scalar2=ROUND_MAGIC, op0=ALU.add, op1=ALU.subtract
         )
-        nc.vector.tensor_tensor(out=turns[:], in0=turns[:], in1=whole[:], op=ALU.subtract)
+        nc.gpsimd.tensor_tensor(out=turns[:], in0=turns[:], in1=whole[:], op=ALU.subtract)
+        cos_sin = keep.tile([P, 2, TILES, HALF], F32)
 
         spread = keep.tile([P, 10 * BANK], BF16)
 
-        def spread_rows(source, row, pair):
+        def spread_rows(source, row, pair, second=BANK):
             copies = psum.tile([P, 2 * BANK], BF16, tag="bank")
-            for i in range(2):
+            for i, width in enumerate((BANK, second)):
                 nc.tensor.matmul(
-                    copies[:, BANK * i : BANK * (i + 1)],
+                    copies[:, BANK * i : BANK * i + width],
                     lhsT=ident_bf16[:, row + i : row + i + 1].to_broadcast([P, P]),
-                    rhs=source[:],
+                    rhs=source[:, 0:width],
                     start=True,
                     stop=True,
                 )
-            nc.scalar.copy(out=spread[:, 2 * BANK * pair : 2 * BANK * (pair + 1)], in_=copies[:])
+            return pair, copies, BANK + second
 
-        x_words = x_raw[:].bitcast(F32)
-        x_codes = keep.tile([P, TILES, PASSES * P], U32, align_bytes=64)
-        x_scales = keep.tile([P, TILES, PASSES * P], U8, align_bytes=64)
+        def keep_spread(engine_copy, pair, copies, width):
+            engine_copy(out=spread[:, 2 * BANK * pair : 2 * BANK * pair + width], in_=copies[:, 0:width])
+
+        x_codes = {}
+        x_scales = {}
 
         def flip(t):
             flipped = psum.tile([P, PASSES, 2, P], F32, tag="bank")
             for g in range(PASSES):
                 for u in range(2):
                     nc.tensor.transpose(
-                        flipped[:, g, u, :], x_words[:, t, 256 * g + u : 256 * (g + 1) : 2], ident_f32[:]
+                        flipped[:, g, u, :], x_words[t][:, 256 * g + u : 256 * (g + 1) : 2], ident_f32[:]
                     )
+            return flipped
+
+        def group(flipped):
             grouped = stage.tile([P, PASSES, P, 4], BF16, align_bytes=64, tag="grouped")
             nc.scalar.copy(out=grouped[:].bitcast(F32), in_=flipped[:].rearrange("p g u r -> p g r u"))
             return grouped
 
         def quantise(t, grouped):
+            x_codes[t] = keep.tile([P, PASSES * P], U32, align_bytes=64, name="x_codes_%d" % t)
+            x_scales[t] = keep.tile([P, PASSES * P], U8, align_bytes=64, name="x_scales_%d" % t)
             nc.vector.quantize_mx(
-                out=x_codes[:, t, :].bitcast(FP8X4),
-                scales=x_scales[:, t, :],
+                out=x_codes[t][:].bitcast(FP8X4),
+                scales=x_scales[t][:],
                 in_=grouped[:].rearrange("p g r j -> p (g r j)"),
             )
 
-        spread_rows(bias_rows, 0, 0)
-        ahead = [flip(0), flip(1)]
-        quantise(0, ahead[0])
-        quantise(1, ahead[1])
-        for pair in range(1, 4):
-            spread_rows(bias_rows, 2 * pair, pair)
-
-        cos_sin = keep.tile([P, 2, TILES, HALF], F32)
-        nc.scalar.activation(out=cos_sin[:], in_=turns[:], func=ACT.Sin, scale=2.0 * math.pi)
-
-
         def project(t, acc, first, width):
             chunk, inside = first // W_CHUNK, first % W_CHUNK
+            plane_first, plane_last, plane = scale_tiles[0 if first < SCALE_SPLIT else 1]
             for g in range(PASSES):
                 nc.tensor.matmul_mx(
                     out=acc,
-                    lhsT=x_codes[:, t, P * g : P * (g + 1)].bitcast(FP8X4),
-                    lhsT_scale=x_scales[:, t, P * g : P * (g + 1)],
+                    lhsT=x_codes[t][:, P * g : P * (g + 1)].bitcast(FP8X4),
+                    lhsT_scale=x_scales[t][:, P * g : P * (g + 1)],
                     rhs=w_words[chunk][:, g, 2 * inside : 2 * (inside + width)].bitcast(FP4X4),
-                    rhs_scale=w_scales[:, g, first : first + width],
+                    rhs_scale=plane[:, g, first - plane_first : first - plane_first + width],
                     start=(g == 0),
                     stop=(g == PASSES - 1),
                 )
@@ -231,7 +254,7 @@ def tile_gau_ae_pa_kernel(
                 nc.gpsimd.tensor_tensor(out=out, in0=left[:], in1=right[:], op=op)
             return first, count, rotated
 
-        def silu_and_store(t, half, first_bank, banks):
+        def silu_and_store(t, half, first_bank, banks, silu_banks=2):
             z = zpool.tile([P, BANK * banks], F32, tag="z%d" % banks)
             for b in range(banks):
                 first = UV * half + BANK * (first_bank + b)
@@ -240,39 +263,73 @@ def tile_gau_ae_pa_kernel(
                 nc.vector.tensor_tensor(
                     out=z[:, BANK * b : BANK * (b + 1)], in0=acc[:], in1=spread[:, first : first + BANK], op=ALU.add
                 )
-            nc.scalar.activation(out=z[:], in_=z[:], func=ACT.Silu)
+                if (b + 1) % silu_banks == 0 or b + 1 == banks:
+                    done = BANK * (b - b % silu_banks)
+                    nc.scalar.activation(
+                        out=z[:, done : BANK * (b + 1)], in_=z[:, done : BANK * (b + 1)], func=ACT.Silu
+                    )
             nc.sync.dma_start(
                 out=uv_dram[half][:, t, BANK * first_bank : BANK * (first_bank + banks)], in_=z[:]
             )
 
+        def store_q_and_k(batch):
+            first, count, rotated = batch
+            for c in range(2):
+                nc.sync.dma_start(out=qk_dram[c][:, first : first + count, :], in_=rotated[:, c, :, :])
+
         banks_of_half = UV // BANK
-        in_work = []
+
+        bias_01 = spread_rows(bias_rows, 0, 0)
+        flipped_0 = flip(0)
+        grouped_0 = group(flipped_0)
+        keep_spread(nc.vector.tensor_copy, *bias_01)
+        bias_23 = spread_rows(bias_rows, 2, 1)
+        quantise(0, grouped_0)
+        keep_spread(nc.vector.tensor_copy, *bias_23)
+        bias_45 = spread_rows(bias_rows, 4, 2)
+        keep_spread(nc.scalar.copy, *bias_45)
+        flipped_1 = flip(1)
+        grouped_1 = group(flipped_1)
+        bias_67 = spread_rows(bias_rows, 6, 3)
+        keep_spread(nc.scalar.copy, *bias_67)
+        silu_and_store(0, 0, 0, 2, 1)
+        quantise(1, grouped_1)
+        silu_and_store(1, 0, 0, 2, 1)
+        silu_and_store(0, 0, 2, 2)
+        silu_and_store(1, 0, 2, 2)
+
+        batches = {}
         for t in range(0, TILES, 2):
             more = t + 2 < TILES
-            silu_and_store(t, 0, 0, banks_of_half)
+            if t > 0:
+                silu_and_store(t, 0, 0, banks_of_half)
             if more:
-                ahead = [flip(t + 2), flip(t + 3)]
-            silu_and_store(t + 1, 0, 0, banks_of_half)
+                flipped = [flip(t + 2), flip(t + 3)]
+                ahead = [group(flipped[0]), group(flipped[1])]
+            if t > 0:
+                silu_and_store(t + 1, 0, 0, banks_of_half)
+            if not more:
+                store_q_and_k(batches[t - 2])
             if t == 0:
-                spread_rows(small_rows, 0, 4)
+                small = spread_rows(small_rows, 0, 4, KEY)
+                keep_spread(nc.scalar.copy, *small)
+                nc.scalar.activation(out=cos_sin[:], in_=turns[:], func=ACT.Sin, scale=2.0 * math.pi)
             silu_and_store(t, 1, 0, banks_of_half)
             if more:
                 quantise(t + 2, ahead[0])
                 quantise(t + 3, ahead[1])
             if t == 0:
-                nc.vector.tensor_copy(
+                nc.gpsimd.tensor_copy(
                     out=halves[:].rearrange("p v (h j) -> p v h j", h=2),
                     in_=spread[:, 2 * UV : 2 * UV + 5 * KEY].rearrange("p (v j h) -> p v h j", v=5, h=2),
                 )
-                first_batch = q_and_k(0, 2)
+                batches[0] = q_and_k(0, 2)
             if more:
                 silu_and_store(t + 1, 1, 0, banks_of_half)
+                if t > 0:
+                    store_q_and_k(batches[t - 2])
+                batches[t + 2] = q_and_k(t + 2, 2)
             else:
+                store_q_and_k(batches[t])
                 for b in range(banks_of_half):
                     silu_and_store(t + 1, 1, b, 1)
-            for first, count, rotated in in_work:
-                for c in range(2):
-                    nc.sync.dma_start(out=qk_dram[c][:, first : first + count, :], in_=rotated[:, c, :, :])
-            in_work = [first_batch] if t == 0 else []
-            if more:
-                in_work.append(q_and_k(t + 2, 2))

@@ -62,20 +62,17 @@ def tile_gau_ae_pa_kernel(
         bias_rows = keep.tile([P, BANK], BF16)
         small_rows = keep.tile([P, BANK], BF16)
         warm = keep.tile([P, 1], F32)
-        zeros = keep.tile([P, BANK], BF16)
         nc.vector.memset(warm[:], 0.0)
         nc.vector.memset(bias_rows[:].bitcast(I32), 0)
-        nc.vector.memset(zeros[:].bitcast(I32), 0)
-        nc.vector.memset(scale_tiles[0][2][:].bitcast(I32), 0)
         nc.vector.memset(small_rows[:].bitcast(I32), 0)
-        nc.vector.memset(scale_tiles[1][2][:].bitcast(I32), 0)
+        nc.vector.memset(scale_tiles[0][2][:].bitcast(I32), 0)
         nc.scalar.dma_start(out=bias_rows[0:8, :], in_=bi[0 : 2 * UV].rearrange("(c n) -> c n", n=BANK))
 
         nc.scalar.activation(out=warm[:], in_=warm[:], func=ACT.Silu)
 
         idle = psum.tile([P, BANK], F32, tag="bank")
         for i in range(WARM_UP):
-            nc.tensor.matmul(idle[:], lhsT=zeros[:, 0:P], rhs=zeros[:], start=True, stop=True)
+            nc.tensor.matmul(idle[:], lhsT=small_rows[:, 0:P], rhs=small_rows[:], start=True, stop=True)
 
         x_words = {}
 
@@ -109,52 +106,52 @@ def tile_gau_ae_pa_kernel(
         load_tokens(1, 1)
         load_weights(1)
         load_tokens(2, 2)
-        load_scales(1)
-        load_weights(2)
-        load_weights(3)
-        load_tokens(4, 2)
-        load_weights(4)
-        for v, vector in enumerate((bi[2 * UV : WI], q_gamma, k_gamma, q_beta, k_beta)):
-            row, slot = v // 4, v % 4
-            nc.sync.dma_start(
-                out=small_rows[row : row + 1, KEY * slot : KEY * (slot + 1)],
-                in_=vector.rearrange("(o n) -> o n", o=1),
-            )
-        load_tokens(6, 2)
+
+        def later_loads():
+            nc.vector.memset(scale_tiles[1][2][:].bitcast(I32), 0)
+            load_scales(1)
+            load_weights(2)
+            load_weights(3)
+            load_tokens(4, 2)
+            load_weights(4)
+            for i, vector in enumerate((bi[2 * UV : WI], q_gamma, k_gamma, q_beta, k_beta)):
+                row, slot = i // 4, i % 4
+                nc.sync.dma_start(
+                    out=small_rows[row : row + 1, KEY * slot : KEY * (slot + 1)],
+                    in_=vector.rearrange("(o n) -> o n", o=1),
+                )
+            load_tokens(6, 2)
 
         ident_bf16 = keep.tile([P, P], BF16)
         nc.vector.tensor_copy(out=ident_bf16[:], in_=ident_f32[:])
+        per_turn = keep.tile([P, HALF], F32)
+        nc.vector.memset(per_turn[:, 0:1], 1.0)
+        nc.vector.tensor_scalar_mul(out=per_turn[:, 0:1], in0=per_turn[:, 0:1], scalar1=1.0 / (2.0 * math.pi))
+        for w in (1, 2, 4, 8, 16, 32):
+            nc.vector.tensor_scalar_mul(
+                out=per_turn[:, w : 2 * w], in0=per_turn[:, 0:w], scalar1=10000.0 ** (-w / HALF)
+            )
         position = keep.tile([P, TILES], F32)
         nc.vector.tensor_copy(out=position[:], in_=position_i[:])
-        per_turn = keep.tile([P, HALF], F32)
-        nc.gpsimd.memset(per_turn[:, 0:1], 1.0)
-        nc.gpsimd.tensor_scalar(
-            out=per_turn[:, 0:1], in0=per_turn[:, 0:1], scalar1=1.0 / (2.0 * math.pi), scalar2=0.0,
-            op0=ALU.mult, op1=ALU.add,
-        )
-        for w in (1, 2, 4, 8, 16, 32):
-            nc.gpsimd.tensor_scalar(
-                out=per_turn[:, w : 2 * w], in0=per_turn[:, 0:w], scalar1=10000.0 ** (-w / HALF), scalar2=0.0,
-                op0=ALU.mult, op1=ALU.add,
-            )
         turns = keep.tile([P, 2, TILES, HALF], F32)
-        nc.gpsimd.tensor_tensor(
+        nc.vector.tensor_tensor(
             out=turns[:, 1, :, :],
             in0=per_turn[:].unsqueeze(1).to_broadcast([P, TILES, HALF]),
             in1=position[:].unsqueeze(2).to_broadcast([P, TILES, HALF]),
             op=ALU.mult,
         )
-        nc.gpsimd.tensor_scalar(
-            out=turns[:, 0, :, :], in0=turns[:, 1, :, :], scalar1=0.25, scalar2=0.0, op0=ALU.add, op1=ALU.add
-        )
+        nc.vector.tensor_scalar_add(out=turns[:, 0, :, :], in0=turns[:, 1, :, :], scalar1=0.25)
         whole = keep.tile([P, 2, TILES, HALF], F32)
-        nc.gpsimd.tensor_scalar(
-            out=whole[:], in0=turns[:], scalar1=ROUND_MAGIC, scalar2=ROUND_MAGIC, op0=ALU.add, op1=ALU.subtract
-        )
-        nc.gpsimd.tensor_tensor(out=turns[:], in0=turns[:], in1=whole[:], op=ALU.subtract)
         cos_sin = keep.tile([P, 2, TILES, HALF], F32)
 
-        spread = keep.tile([P, 10 * BANK], BF16)
+        def cos_and_sin():
+            nc.vector.tensor_scalar(
+                out=whole[:], in0=turns[:], scalar1=ROUND_MAGIC, scalar2=ROUND_MAGIC, op0=ALU.add, op1=ALU.subtract
+            )
+            nc.vector.tensor_tensor(out=turns[:], in0=turns[:], in1=whole[:], op=ALU.subtract)
+            nc.scalar.activation(out=cos_sin[:], in_=turns[:], func=ACT.Sin, scale=2.0 * math.pi)
+
+        spread = keep.tile([P, 2 * UV], BF16)
 
         def spread_rows(source, row, pair, second=BANK):
             copies = psum.tile([P, 2 * BANK], BF16, tag="bank")
@@ -286,6 +283,7 @@ def tile_gau_ae_pa_kernel(
         bias_23 = spread_rows(bias_rows, 2, 1)
         quantise(0, grouped_0)
         keep_spread(nc.vector.tensor_copy, *bias_23)
+        later_loads()
         bias_45 = spread_rows(bias_rows, 4, 2)
         keep_spread(nc.scalar.copy, *bias_45)
         flipped_1 = flip(1)
@@ -311,17 +309,16 @@ def tile_gau_ae_pa_kernel(
             if not more:
                 store_q_and_k(batches[t - 2])
             if t == 0:
-                small = spread_rows(small_rows, 0, 4, KEY)
-                keep_spread(nc.scalar.copy, *small)
-                nc.scalar.activation(out=cos_sin[:], in_=turns[:], func=ACT.Sin, scale=2.0 * math.pi)
+                cos_and_sin()
             silu_and_store(t, 1, 0, banks_of_half)
             if more:
                 quantise(t + 2, ahead[0])
                 quantise(t + 3, ahead[1])
             if t == 0:
-                nc.gpsimd.tensor_copy(
+                small = spread_rows(small_rows, 0, 4, KEY)[1]
+                nc.vector.tensor_copy(
                     out=halves[:].rearrange("p v (h j) -> p v h j", h=2),
-                    in_=spread[:, 2 * UV : 2 * UV + 5 * KEY].rearrange("p (v j h) -> p v h j", v=5, h=2),
+                    in_=small[:, 0 : 5 * KEY].rearrange("p (v j h) -> p v h j", v=5, h=2),
                 )
                 batches[0] = q_and_k(0, 2)
             if more:

@@ -25,9 +25,11 @@ TILES = TOKENS // P
 K_PASS = 4 * P
 PASSES = DIM // K_PASS
 BANK = 512
-W_CHUNK = 1024
-SCALE_SPLIT = UV
+W_EDGES = (0, 512, 1024, 1536, 2048, 3072, 2 * UV, WI)
+SCALE_EDGES = (0, 1024, UV, WI)
+RUN = UV // P
 WARM_UP = 4
+FAST = 46
 ROUND_MAGIC = 1.5 * 2.0**23
 
 FLOPS = 2 * TOKENS * DIM * WI
@@ -56,23 +58,32 @@ def tile_gau_ae_pa_kernel(
         nc.gpsimd.iota(position_i[:], pattern=[[1, TILES]], base=0, channel_multiplier=TILES)
 
         scale_tiles = []
-        for i, (first, last) in enumerate(((0, SCALE_SPLIT), (SCALE_SPLIT, WI))):
+        for i, (first, last) in enumerate(zip(SCALE_EDGES, SCALE_EDGES[1:])):
             plane = keep.tile([P, PASSES, last - first], U8, align_bytes=64, name="w_scales_%d" % i)
             scale_tiles.append((first, last, plane))
-        bias_rows = keep.tile([P, BANK], BF16)
+        bias_cols = keep.tile([P, 2, RUN], BF16)
         small_rows = keep.tile([P, BANK], BF16)
         warm = keep.tile([P, 1], F32)
+        zeros = keep.tile([P, BANK], BF16)
+        nc.gpsimd.memset(small_rows[:].bitcast(I32), 0)
         nc.vector.memset(warm[:], 0.0)
-        nc.vector.memset(bias_rows[:].bitcast(I32), 0)
-        nc.vector.memset(small_rows[:].bitcast(I32), 0)
         nc.vector.memset(scale_tiles[0][2][:].bitcast(I32), 0)
-        nc.scalar.dma_start(out=bias_rows[0:8, :], in_=bi[0 : 2 * UV].rearrange("(c n) -> c n", n=BANK))
+        nc.vector.memset(zeros[:].bitcast(I32), 0)
+        nc.vector.memset(scale_tiles[1][2][:].bitcast(I32), 0)
+        nc.scalar.dma_start(out=bias_cols[:], in_=bi[0 : 2 * UV].rearrange("(h n r) -> n h r", h=2, r=RUN))
+
+        for i, vector in enumerate((bi[2 * UV : WI], q_gamma, k_gamma, q_beta, k_beta)):
+            row, slot = i // 4, i % 4
+            nc.gpsimd.dma_start(
+                out=small_rows[row : row + 1, KEY * slot : KEY * (slot + 1)],
+                in_=vector.rearrange("(o n) -> o n", o=1),
+            )
 
         nc.scalar.activation(out=warm[:], in_=warm[:], func=ACT.Silu)
 
         idle = psum.tile([P, BANK], F32, tag="bank")
         for i in range(WARM_UP):
-            nc.tensor.matmul(idle[:], lhsT=small_rows[:, 0:P], rhs=small_rows[:], start=True, stop=True)
+            nc.tensor.matmul(idle[:], lhsT=zeros[:, 0:P], rhs=zeros[:], start=True, stop=True)
 
         x_words = {}
 
@@ -86,7 +97,7 @@ def tile_gau_ae_pa_kernel(
         w_words = {}
 
         def load_weights(chunk):
-            first, last = W_CHUNK * chunk, min(W_CHUNK * (chunk + 1), WI)
+            first, last = W_EDGES[chunk], W_EDGES[chunk + 1]
             w_words[chunk] = keep.tile([P, PASSES, 2 * (last - first)], U8, align_bytes=64, name="w_words_%d" % chunk)
             nc.sync.dma_start(
                 out=w_words[chunk][:].bitcast(I32), in_=w_dram[:, :, 2 * first : 2 * last].bitcast(I32)
@@ -103,24 +114,20 @@ def tile_gau_ae_pa_kernel(
         load_tokens(0, 1)
         load_scales(0)
         load_weights(0)
-        load_tokens(1, 1)
         load_weights(1)
+        load_tokens(1, 1)
+        load_scales(1)
+        load_weights(2)
+        load_weights(3)
         load_tokens(2, 2)
 
         def later_loads():
-            nc.vector.memset(scale_tiles[1][2][:].bitcast(I32), 0)
-            load_scales(1)
-            load_weights(2)
-            load_weights(3)
-            load_tokens(4, 2)
+            nc.vector.memset(scale_tiles[2][2][:].bitcast(I32), 0)
+            load_scales(2)
+            load_weights(6)
             load_weights(4)
-            for i, vector in enumerate((bi[2 * UV : WI], q_gamma, k_gamma, q_beta, k_beta)):
-                row, slot = i // 4, i % 4
-                nc.sync.dma_start(
-                    out=small_rows[row : row + 1, KEY * slot : KEY * (slot + 1)],
-                    in_=vector.rearrange("(o n) -> o n", o=1),
-                )
-            load_tokens(6, 2)
+            load_weights(5)
+            load_tokens(4, 4)
 
         ident_bf16 = keep.tile([P, P], BF16)
         nc.vector.tensor_copy(out=ident_bf16[:], in_=ident_f32[:])
@@ -140,15 +147,18 @@ def tile_gau_ae_pa_kernel(
             in1=position[:].unsqueeze(2).to_broadcast([P, TILES, HALF]),
             op=ALU.mult,
         )
-        nc.vector.tensor_scalar_add(out=turns[:, 0, :, :], in0=turns[:, 1, :, :], scalar1=0.25)
-        whole = keep.tile([P, 2, TILES, HALF], F32)
+        whole = keep.tile([P, 2, TILES, FAST], F32)
         cos_sin = keep.tile([P, 2, TILES, HALF], F32)
 
-        def cos_and_sin():
+        def release_angles():
+            nc.vector.tensor_scalar_add(out=turns[:, 0, :, :], in0=turns[:, 1, :, :], scalar1=0.25)
+            fast = turns[:, :, :, 0:FAST]
             nc.vector.tensor_scalar(
-                out=whole[:], in0=turns[:], scalar1=ROUND_MAGIC, scalar2=ROUND_MAGIC, op0=ALU.add, op1=ALU.subtract
+                out=whole[:], in0=fast, scalar1=ROUND_MAGIC, scalar2=ROUND_MAGIC, op0=ALU.add, op1=ALU.subtract
             )
-            nc.vector.tensor_tensor(out=turns[:], in0=turns[:], in1=whole[:], op=ALU.subtract)
+            nc.vector.tensor_tensor(out=fast, in0=fast, in1=whole[:], op=ALU.subtract)
+
+        def cos_and_sin():
             nc.scalar.activation(out=cos_sin[:], in_=turns[:], func=ACT.Sin, scale=2.0 * math.pi)
 
         spread = keep.tile([P, 2 * UV], BF16)
@@ -165,8 +175,19 @@ def tile_gau_ae_pa_kernel(
                 )
             return pair, copies, BANK + second
 
-        def keep_spread(engine_copy, pair, copies, width):
-            engine_copy(out=spread[:, 2 * BANK * pair : 2 * BANK * pair + width], in_=copies[:, 0:width])
+        bias_words = bias_cols[:].rearrange("p h r -> p (h r)").bitcast(F32)
+
+        def spread_bias(part):
+            copies = psum.tile([P, 4, P], F32, tag="bank")
+            for i in range(4):
+                w = 4 * part + i
+                nc.tensor.transpose(copies[:, i, :], bias_words[:, w : w + 1].to_broadcast([P, P]), ident_f32[:])
+            return part, copies
+
+        def keep_bias(engine_copy, part, copies):
+            half, place = part // 2, part % 2
+            words = spread[:, UV * half : UV * (half + 1)].bitcast(F32).rearrange("p (n w) -> p n w", n=P)
+            engine_copy(out=words[:, :, 4 * place : 4 * place + 4], in_=copies[:].rearrange("p w n -> p n w"))
 
         x_codes = {}
         x_scales = {}
@@ -195,8 +216,9 @@ def tile_gau_ae_pa_kernel(
             )
 
         def project(t, acc, first, width):
-            chunk, inside = first // W_CHUNK, first % W_CHUNK
-            plane_first, plane_last, plane = scale_tiles[0 if first < SCALE_SPLIT else 1]
+            chunk = max(c for c in w_words if W_EDGES[c] <= first)
+            inside = first - W_EDGES[chunk]
+            plane_first, plane = [(start, plane) for start, end, plane in scale_tiles if start <= first][-1]
             for g in range(PASSES):
                 nc.tensor.matmul_mx(
                     out=acc,
@@ -210,7 +232,7 @@ def tile_gau_ae_pa_kernel(
 
         halves = keep.tile([P, 5, KEY], F32)
 
-        def q_and_k(first, count):
+        def qk_front(first, count):
             acc_qk = psum.tile([P, count, KEY], F32, tag="bank")
             for i in range(count):
                 project(first + i, acc_qk[:, i, :], 2 * UV, KEY)
@@ -221,6 +243,9 @@ def tile_gau_ae_pa_kernel(
                 in1=halves[:, 0:1, :].to_broadcast([P, count, KEY]).rearrange("p t (h j) -> p t h j", h=2),
                 op=ALU.add,
             )
+            return first, count, qk
+
+        def qk_back(first, count, qk):
             nc.scalar.activation(out=qk[:], in_=qk[:], func=ACT.Silu)
             scaled = qkpool.tile([P, count, 2, KEY], F32, tag="scaled")
             nc.gpsimd.tensor_tensor(
@@ -251,9 +276,30 @@ def tile_gau_ae_pa_kernel(
                 nc.gpsimd.tensor_tensor(out=out, in0=left[:], in1=right[:], op=op)
             return first, count, rotated
 
-        def silu_and_store(t, half, first_bank, banks, silu_banks=2):
+        def new_z(banks):
+            z = zpool.tile([P, BANK * banks], F32, tag="z%d" % banks)
+            return z
+
+        def bank(z, b, t, half, column_bank):
+            first = UV * half + BANK * column_bank
+            acc = psum.tile([P, BANK], F32, tag="bank")
+            project(t, acc[:], first, BANK)
+            nc.vector.tensor_tensor(
+                out=z[:, BANK * b : BANK * (b + 1)], in0=acc[:], in1=spread[:, first : first + BANK], op=ALU.add
+            )
+
+        def silu(z, b, count=1):
+            part = z[:, BANK * b : BANK * (b + count)]
+            nc.scalar.activation(out=part, in_=part, func=ACT.Silu)
+
+        def store(z, t, half, column_bank, banks):
+            nc.sync.dma_start(out=uv_dram[half][:, t, BANK * column_bank : BANK * (column_bank + banks)], in_=z[:])
+
+        def silu_and_store(t, half, first_bank, banks, silu_banks=2, between=None):
             z = zpool.tile([P, BANK * banks], F32, tag="z%d" % banks)
             for b in range(banks):
+                if between and b in between:
+                    between[b]()
                 first = UV * half + BANK * (first_bank + b)
                 acc = psum.tile([P, BANK], F32, tag="bank")
                 project(t, acc[:], first, BANK)
@@ -276,57 +322,78 @@ def tile_gau_ae_pa_kernel(
 
         banks_of_half = UV // BANK
 
-        bias_01 = spread_rows(bias_rows, 0, 0)
+        batches = {}
+        ahead = {}
+
+        def prepare(*tiles):
+            flipped = [flip(t) for t in tiles]
+            for t, f in zip(tiles, flipped):
+                ahead[t] = group(f)
+
+        def quantise_ahead(*tiles):
+            for t in tiles:
+                quantise(t, ahead[t])
+
+        def batch(t):
+            batches[t] = qk_back(*qk_front(t, 2))
+
+        def spread_small():
+            small = spread_rows(small_rows, 0, 4, KEY)[1]
+            nc.vector.tensor_copy(
+                out=halves[:].rearrange("p v (h j) -> p v h j", h=2),
+                in_=small[:, 0 : 5 * KEY].rearrange("p (v j h) -> p v h j", v=5, h=2),
+            )
+
+        U, V4 = 0, 1
+        bias = [spread_bias(0)]
         flipped_0 = flip(0)
         grouped_0 = group(flipped_0)
-        keep_spread(nc.vector.tensor_copy, *bias_01)
-        bias_23 = spread_rows(bias_rows, 2, 1)
+        bias += [spread_bias(part) for part in (1, 2, 3)]
         quantise(0, grouped_0)
-        keep_spread(nc.vector.tensor_copy, *bias_23)
+        keep_bias(nc.vector.tensor_copy, *bias[0])
+        for part in bias[1:]:
+            keep_bias(nc.scalar.copy, *part)
         later_loads()
-        bias_45 = spread_rows(bias_rows, 4, 2)
-        keep_spread(nc.scalar.copy, *bias_45)
-        flipped_1 = flip(1)
-        grouped_1 = group(flipped_1)
-        bias_67 = spread_rows(bias_rows, 6, 3)
-        keep_spread(nc.scalar.copy, *bias_67)
-        silu_and_store(0, 0, 0, 2, 1)
-        quantise(1, grouped_1)
-        silu_and_store(1, 0, 0, 2, 1)
-        silu_and_store(0, 0, 2, 2)
-        silu_and_store(1, 0, 2, 2)
-
-        batches = {}
-        for t in range(0, TILES, 2):
-            more = t + 2 < TILES
-            if t > 0:
-                silu_and_store(t, 0, 0, banks_of_half)
-            if more:
-                flipped = [flip(t + 2), flip(t + 3)]
-                ahead = [group(flipped[0]), group(flipped[1])]
-            if t > 0:
-                silu_and_store(t + 1, 0, 0, banks_of_half)
-            if not more:
-                store_q_and_k(batches[t - 2])
-            if t == 0:
-                cos_and_sin()
-            silu_and_store(t, 1, 0, banks_of_half)
-            if more:
-                quantise(t + 2, ahead[0])
-                quantise(t + 3, ahead[1])
-            if t == 0:
-                small = spread_rows(small_rows, 0, 4, KEY)[1]
-                nc.vector.tensor_copy(
-                    out=halves[:].rearrange("p v (h j) -> p v h j", h=2),
-                    in_=small[:, 0 : 5 * KEY].rearrange("p (v j h) -> p v h j", v=5, h=2),
-                )
-                batches[0] = q_and_k(0, 2)
-            if more:
-                silu_and_store(t + 1, 1, 0, banks_of_half)
-                if t > 0:
-                    store_q_and_k(batches[t - 2])
-                batches[t + 2] = q_and_k(t + 2, 2)
-            else:
-                store_q_and_k(batches[t])
-                for b in range(banks_of_half):
-                    silu_and_store(t + 1, 1, b, 1)
+        z = new_z(2)
+        bank(z, 0, 0, 0, 0)
+        bank(z, 1, 0, 0, 1)
+        silu(z, 0)
+        release_angles()
+        prepare(1)
+        silu(z, 1)
+        cos_and_sin()
+        store(z, 0, 0, 0, 2)
+        z = new_z(2)
+        bank(z, 0, 0, 0, 2)
+        quantise_ahead(1)
+        bank(z, 1, 0, 0, 3)
+        silu(z, 0)
+        silu(z, 1)
+        store(z, 0, 0, 2, 2)
+        spread_small()
+        silu_and_store(1, 0, 0, 4)
+        front = qk_front(0, 2)
+        prepare(2, 3)
+        batches[0] = qk_back(*front)
+        silu_and_store(0, V4, 0, 4, 2, {2: lambda: quantise_ahead(2, 3)})
+        silu_and_store(1, V4, 0, 4)
+        prepare(4, 5)
+        silu_and_store(2, U, 0, 4)
+        silu_and_store(3, U, 0, 4, 2, {0: lambda: (quantise_ahead(4, 5), batch(2))})
+        store_q_and_k(batches[0])
+        silu_and_store(2, V4, 0, 4)
+        prepare(6, 7)
+        silu_and_store(3, V4, 0, 4)
+        silu_and_store(4, U, 0, 4, 2, {0: lambda: (quantise_ahead(6, 7), batch(4))})
+        store_q_and_k(batches[2])
+        silu_and_store(5, U, 0, 4)
+        silu_and_store(4, V4, 0, 4)
+        batch(6)
+        silu_and_store(5, V4, 0, 4)
+        store_q_and_k(batches[4])
+        silu_and_store(6, U, 0, 4)
+        silu_and_store(7, U, 0, 4)
+        silu_and_store(6, V4, 0, 4)
+        store_q_and_k(batches[6])
+        for b in range(4):
+            silu_and_store(7, V4, b, 1)

@@ -156,6 +156,9 @@ def tile_gau_ae_pa_kernel(
             nc.vector.tensor_scalar(
                 out=whole[:], in0=fast, scalar1=ROUND_MAGIC, scalar2=ROUND_MAGIC, op0=ALU.add, op1=ALU.subtract
             )
+
+        def angles_2():
+            fast = turns[:, :, :, 0:FAST]
             nc.vector.tensor_tensor(out=fast, in0=fast, in1=whole[:], op=ALU.subtract)
 
         def cos_and_sin():
@@ -361,17 +364,17 @@ def tile_gau_ae_pa_kernel(
         release_angles()
         prepare(1)
         silu(z, 1)
-        cos_and_sin()
         store(z, 0, 0, 0, 2)
         z = new_z(2)
-        bank(z, 0, 0, 0, 2)
         quantise_ahead(1)
+        bank(z, 0, 0, 0, 2)
+        angles_2()
         bank(z, 1, 0, 0, 3)
         silu(z, 0)
         silu(z, 1)
         store(z, 0, 0, 2, 2)
-        spread_small()
-        silu_and_store(1, 0, 0, 4)
+        cos_and_sin()
+        silu_and_store(1, 0, 0, 4, 2, {2: spread_small})
         front = qk_front(0, 2)
         prepare(2, 3)
         batches[0] = qk_back(*front)
@@ -395,5 +398,5 @@ def tile_gau_ae_pa_kernel(
         silu_and_store(7, U, 0, 4)
         silu_and_store(6, V4, 0, 4)
         store_q_and_k(batches[6])
-        for b in range(4):
-            silu_and_store(7, V4, b, 1)
+        silu_and_store(7, V4, 0, 2)
+        silu_and_store(7, V4, 2, 2)

@@ -25,9 +25,8 @@ TILES = TOKENS // P
 K_PASS = 4 * P
 PASSES = DIM // K_PASS
 BANK = 512
-W_EDGES = (0, 512, 1024, 1536, 2048, 3072, 2 * UV, WI)
+W_EDGES = (0, 1024, 2048, 3072, 2 * UV, WI)
 SCALE_EDGES = (0, 1024, UV, WI)
-RUN = UV // P
 WARM_UP = 4
 FAST = 46
 ROUND_MAGIC = 1.5 * 2.0**23
@@ -61,16 +60,17 @@ def tile_gau_ae_pa_kernel(
         for i, (first, last) in enumerate(zip(SCALE_EDGES, SCALE_EDGES[1:])):
             plane = keep.tile([P, PASSES, last - first], U8, align_bytes=64, name="w_scales_%d" % i)
             scale_tiles.append((first, last, plane))
-        bias_cols = keep.tile([P, 2, RUN], BF16)
+        bias_rows = keep.tile([P, BANK], BF16)
         small_rows = keep.tile([P, BANK], BF16)
         warm = keep.tile([P, 1], F32)
         zeros = keep.tile([P, BANK], BF16)
         nc.gpsimd.memset(small_rows[:].bitcast(I32), 0)
         nc.vector.memset(warm[:], 0.0)
+        nc.vector.memset(bias_rows[:].bitcast(I32), 0)
         nc.vector.memset(scale_tiles[0][2][:].bitcast(I32), 0)
         nc.vector.memset(zeros[:].bitcast(I32), 0)
         nc.vector.memset(scale_tiles[1][2][:].bitcast(I32), 0)
-        nc.scalar.dma_start(out=bias_cols[:], in_=bi[0 : 2 * UV].rearrange("(h n r) -> n h r", h=2, r=RUN))
+        nc.scalar.dma_start(out=bias_rows[0:8, :], in_=bi[0 : 2 * UV].rearrange("(c n) -> c n", n=BANK))
 
         for i, vector in enumerate((bi[2 * UV : WI], q_gamma, k_gamma, q_beta, k_beta)):
             row, slot = i // 4, i % 4
@@ -114,19 +114,17 @@ def tile_gau_ae_pa_kernel(
         load_tokens(0, 1)
         load_scales(0)
         load_weights(0)
-        load_weights(1)
         load_tokens(1, 1)
         load_scales(1)
-        load_weights(2)
-        load_weights(3)
+        load_weights(1)
         load_tokens(2, 2)
 
         def later_loads():
             nc.vector.memset(scale_tiles[2][2][:].bitcast(I32), 0)
             load_scales(2)
-            load_weights(6)
             load_weights(4)
-            load_weights(5)
+            load_weights(2)
+            load_weights(3)
             load_tokens(4, 4)
 
         ident_bf16 = keep.tile([P, P], BF16)
@@ -178,19 +176,8 @@ def tile_gau_ae_pa_kernel(
                 )
             return pair, copies, BANK + second
 
-        bias_words = bias_cols[:].rearrange("p h r -> p (h r)").bitcast(F32)
-
-        def spread_bias(part):
-            copies = psum.tile([P, 4, P], F32, tag="bank")
-            for i in range(4):
-                w = 4 * part + i
-                nc.tensor.transpose(copies[:, i, :], bias_words[:, w : w + 1].to_broadcast([P, P]), ident_f32[:])
-            return part, copies
-
-        def keep_bias(engine_copy, part, copies):
-            half, place = part // 2, part % 2
-            words = spread[:, UV * half : UV * (half + 1)].bitcast(F32).rearrange("p (n w) -> p n w", n=P)
-            engine_copy(out=words[:, :, 4 * place : 4 * place + 4], in_=copies[:].rearrange("p w n -> p n w"))
+        def keep_spread(engine_copy, pair, copies, width):
+            engine_copy(out=spread[:, 2 * BANK * pair : 2 * BANK * pair + width], in_=copies[:, 0:width])
 
         x_codes = {}
         x_scales = {}
@@ -348,14 +335,13 @@ def tile_gau_ae_pa_kernel(
             )
 
         U, V4 = 0, 1
-        bias = [spread_bias(0)]
         flipped_0 = flip(0)
         grouped_0 = group(flipped_0)
-        bias += [spread_bias(part) for part in (1, 2, 3)]
+        bias_01 = spread_rows(bias_rows, 0, 0)
+        bias_23 = spread_rows(bias_rows, 2, 1)
         quantise(0, grouped_0)
-        keep_bias(nc.vector.tensor_copy, *bias[0])
-        for part in bias[1:]:
-            keep_bias(nc.scalar.copy, *part)
+        keep_spread(nc.vector.tensor_copy, *bias_01)
+        keep_spread(nc.scalar.copy, *bias_23)
         later_loads()
         z = new_z(2)
         bank(z, 0, 0, 0, 0)
@@ -363,8 +349,12 @@ def tile_gau_ae_pa_kernel(
         silu(z, 0)
         release_angles()
         prepare(1)
+        bias_45 = spread_rows(bias_rows, 4, 2)
+        bias_67 = spread_rows(bias_rows, 6, 3)
         silu(z, 1)
         store(z, 0, 0, 0, 2)
+        keep_spread(nc.scalar.copy, *bias_45)
+        keep_spread(nc.scalar.copy, *bias_67)
         z = new_z(2)
         quantise_ahead(1)
         bank(z, 0, 0, 0, 2)
@@ -382,12 +372,14 @@ def tile_gau_ae_pa_kernel(
         silu_and_store(1, V4, 0, 4)
         prepare(4, 5)
         silu_and_store(2, U, 0, 4)
-        silu_and_store(3, U, 0, 4, 2, {0: lambda: (quantise_ahead(4, 5), batch(2))})
+        silu_and_store(3, U, 0, 4, 2, {2: lambda: (quantise_ahead(4, 5), batch(2))})
         store_q_and_k(batches[0])
         silu_and_store(2, V4, 0, 4)
         prepare(6, 7)
         silu_and_store(3, V4, 0, 4)
-        silu_and_store(4, U, 0, 4, 2, {0: lambda: (quantise_ahead(6, 7), batch(4))})
+        silu_and_store(4, U, 0, 4)
+        quantise_ahead(6, 7)
+        batch(4)
         store_q_and_k(batches[2])
         silu_and_store(5, U, 0, 4)
         silu_and_store(4, V4, 0, 4)

@@ -364,31 +364,32 @@ def tile_gau_ae_pa_kernel(
         silu(z, 1)
         store(z, 0, 0, 2, 2)
         cos_and_sin()
-        silu_and_store(1, 0, 0, 4, 2, {2: spread_small})
-        front = qk_front(0, 2)
+        silu_and_store(1, 0, 0, 4)
         prepare(2, 3)
+        spread_small()
+        front = qk_front(0, 2)
         batches[0] = qk_back(*front)
         silu_and_store(0, V4, 0, 4, 2, {2: lambda: quantise_ahead(2, 3)})
         silu_and_store(1, V4, 0, 4)
         prepare(4, 5)
         silu_and_store(2, U, 0, 4)
         silu_and_store(3, U, 0, 4, 2, {2: lambda: (quantise_ahead(4, 5), batch(2))})
-        store_q_and_k(batches[0])
         silu_and_store(2, V4, 0, 4)
+        store_q_and_k(batches[0])
         prepare(6, 7)
         silu_and_store(3, V4, 0, 4)
         silu_and_store(4, U, 0, 4)
         quantise_ahead(6, 7)
         batch(4)
-        store_q_and_k(batches[2])
         silu_and_store(5, U, 0, 4)
+        store_q_and_k(batches[2])
         silu_and_store(4, V4, 0, 4)
         batch(6)
         silu_and_store(5, V4, 0, 4)
-        store_q_and_k(batches[4])
         silu_and_store(6, U, 0, 4)
+        store_q_and_k(batches[4])
         silu_and_store(7, U, 0, 4)
         silu_and_store(6, V4, 0, 4)
-        store_q_and_k(batches[6])
         silu_and_store(7, V4, 0, 2)
+        store_q_and_k(batches[6])
         silu_and_store(7, V4, 2, 2)

@@ -72,13 +72,6 @@ def tile_gau_ae_pa_kernel(
         nc.vector.memset(scale_tiles[1][2][:].bitcast(I32), 0)
         nc.scalar.dma_start(out=bias_rows[0:8, :], in_=bi[0 : 2 * UV].rearrange("(c n) -> c n", n=BANK))
 
-        for i, vector in enumerate((bi[2 * UV : WI], q_gamma, k_gamma, q_beta, k_beta)):
-            row, slot = i // 4, i % 4
-            nc.gpsimd.dma_start(
-                out=small_rows[row : row + 1, KEY * slot : KEY * (slot + 1)],
-                in_=vector.rearrange("(o n) -> o n", o=1),
-            )
-
         nc.scalar.activation(out=warm[:], in_=warm[:], func=ACT.Silu)
 
         idle = psum.tile([P, BANK], F32, tag="bank")
@@ -124,6 +117,12 @@ def tile_gau_ae_pa_kernel(
             load_scales(2)
             load_weights(4)
             load_weights(2)
+            for i, vector in enumerate((bi[2 * UV : WI], q_gamma, k_gamma, q_beta, k_beta)):
+                row, slot = i // 4, i % 4
+                nc.sync.dma_start(
+                    out=small_rows[row : row + 1, KEY * slot : KEY * (slot + 1)],
+                    in_=vector.rearrange("(o n) -> o n", o=1),
+                )
             load_weights(3)
             load_tokens(4, 4)
 

import math
from contextlib import ExitStack

import concourse.mybir as mybir
from concourse.masks import make_identity

F32 = mybir.dt.float32
BF16 = mybir.dt.bfloat16
I32 = mybir.dt.int32
U32 = mybir.dt.uint32
U8 = mybir.dt.uint8
FP8X4 = mybir.dt.float8_e4m3fn_x4
FP4X4 = mybir.dt.float4_e2m1fn_x4
ALU = mybir.AluOpType
ACT = mybir.ActivationFunctionType

P = 128
TOKENS = 1024
DIM = 1024
UV = 2048
KEY = 128
HALF = KEY // 2
WI = 2 * UV + KEY
TILES = TOKENS // P
K_PASS = 4 * P
PASSES = DIM // K_PASS
BANK = 512
W_EDGES = (0, 1024, 2048, 3072, 2 * UV, WI)
SCALE_EDGES = (0, 1024, UV, WI)
WARM_UP = 4
FAST = 46
ROUND_MAGIC = 1.5 * 2.0**23

FLOPS = 2 * TOKENS * DIM * WI


def tile_gau_ae_pa_kernel(
    tc, hidden_states, Wi_words, Wi_scales, bi, q_gamma, q_beta, k_gamma, k_beta, out_0, out_1, out_2, out_3
):
    nc = tc.nc
    x_dram = hidden_states.flatten_outer_dims().rearrange("(p t) k -> p t k", t=TILES)
    uv_dram = [o.flatten_outer_dims().rearrange("(p t) n -> p t n", t=TILES) for o in (out_0, out_1)]
    qk_dram = [o.flatten_outer_dims().rearrange("(p t) f -> p t f", t=TILES) for o in (out_2, out_3)]

    with ExitStack() as ctx:
        keep = ctx.enter_context(tc.tile_pool(name="keep", bufs=1))
        stage = ctx.enter_context(tc.tile_pool(name="stage", bufs=4))
        zpool = ctx.enter_context(tc.tile_pool(name="zpool", bufs=6))
        qkpool = ctx.enter_context(tc.tile_pool(name="qkpool", bufs=3))
        psum = ctx.enter_context(tc.psum_pool(name="psum", bufs=8))

        ctx.enter_context(tc.manual_schedule())

        ident_f32 = keep.tile([P, P], F32)
        make_identity(nc, ident_f32[:])
        position_i = keep.tile([P, TILES], I32)
        nc.gpsimd.iota(position_i[:], pattern=[[1, TILES]], base=0, channel_multiplier=TILES)

        scale_tiles = []
        for i, (first, last) in enumerate(zip(SCALE_EDGES, SCALE_EDGES[1:])):
            plane = keep.tile([P, PASSES, last - first], U8, align_bytes=64, name="w_scales_%d" % i)
            scale_tiles.append((first, last, plane))
        bias_rows = keep.tile([P, BANK], BF16)
        small_rows = keep.tile([P, BANK], BF16)
        warm = keep.tile([P, 1], F32)
        zeros = keep.tile([P, BANK], BF16)
        nc.gpsimd.memset(small_rows[:].bitcast(I32), 0)
        nc.vector.memset(warm[:], 0.0)
        nc.vector.memset(bias_rows[:].bitcast(I32), 0)
        nc.vector.memset(scale_tiles[0][2][:].bitcast(I32), 0)
        nc.vector.memset(zeros[:].bitcast(I32), 0)
        nc.vector.memset(scale_tiles[1][2][:].bitcast(I32), 0)
        nc.scalar.dma_start(out=bias_rows[0:8, :], in_=bi[0 : 2 * UV].rearrange("(c n) -> c n", n=BANK))

        nc.scalar.activation(out=warm[:], in_=warm[:], func=ACT.Silu)

        idle = psum.tile([P, BANK], F32, tag="bank")
        for i in range(WARM_UP):
            nc.tensor.matmul(idle[:], lhsT=zeros[:, 0:P], rhs=zeros[:], start=True, stop=True)

        x_words = {}

        def load_tokens(t, count):
            x_raw = keep.tile([P, count, DIM], BF16, name="x_raw_%d" % t)
            nc.sync.dma_start(out=x_raw[:], in_=x_dram[:, t : t + count, :])
            for i in range(count):
                x_words[t + i] = x_raw[:, i, :].bitcast(F32)

        w_dram = Wi_words.rearrange("g p b -> p g b")
        w_words = {}

        def load_weights(chunk):
            first, last = W_EDGES[chunk], W_EDGES[chunk + 1]
            w_words[chunk] = keep.tile([P, PASSES, 2 * (last - first)], U8, align_bytes=64, name="w_words_%d" % chunk)
            nc.sync.dma_start(
                out=w_words[chunk][:].bitcast(I32), in_=w_dram[:, :, 2 * first : 2 * last].bitcast(I32)
            )

        def load_scales(i):
            first, last, plane = scale_tiles[i]
            for r in range(4):
                nc.sync.dma_start(
                    out=plane[r:P:32, :, :].bitcast(I32),
                    in_=Wi_scales[:, r:16:4, first:last].rearrange("g q n -> q g n").bitcast(I32),
                )

        load_tokens(0, 1)
        load_scales(0)
        load_weights(0)
        load_tokens(1, 1)
        load_scales(1)
        load_weights(1)
        load_tokens(2, 2)

        def later_loads():
            nc.vector.memset(scale_tiles[2][2][:].bitcast(I32), 0)
            load_scales(2)
            load_weights(4)
            load_weights(2)
            for i, vector in enumerate((bi[2 * UV : WI], q_gamma, k_gamma, q_beta, k_beta)):
                row, slot = i // 4, i % 4
                nc.sync.dma_start(
                    out=small_rows[row : row + 1, KEY * slot : KEY * (slot + 1)],
                    in_=vector.rearrange("(o n) -> o n", o=1),
                )
            load_weights(3)
            load_tokens(4, 4)

        ident_bf16 = keep.tile([P, P], BF16)
        nc.vector.tensor_copy(out=ident_bf16[:], in_=ident_f32[:])
        per_turn = keep.tile([P, HALF], F32)
        nc.vector.memset(per_turn[:, 0:1], 1.0)
        nc.vector.tensor_scalar_mul(out=per_turn[:, 0:1], in0=per_turn[:, 0:1], scalar1=1.0 / (2.0 * math.pi))
        for w in (1, 2, 4, 8, 16, 32):
            nc.vector.tensor_scalar_mul(
                out=per_turn[:, w : 2 * w], in0=per_turn[:, 0:w], scalar1=10000.0 ** (-w / HALF)
            )
        position = keep.tile([P, TILES], F32)
        nc.vector.tensor_copy(out=position[:], in_=position_i[:])
        turns = keep.tile([P, 2, TILES, HALF], F32)
        nc.vector.tensor_tensor(
            out=turns[:, 1, :, :],
            in0=per_turn[:].unsqueeze(1).to_broadcast([P, TILES, HALF]),
            in1=position[:].unsqueeze(2).to_broadcast([P, TILES, HALF]),
            op=ALU.mult,
        )
        whole = keep.tile([P, 2, TILES, FAST], F32)
        cos_sin = keep.tile([P, 2, TILES, HALF], F32)

        def release_angles():
            nc.vector.tensor_scalar_add(out=turns[:, 0, :, :], in0=turns[:, 1, :, :], scalar1=0.25)
            fast = turns[:, :, :, 0:FAST]
            nc.vector.tensor_scalar(
                out=whole[:], in0=fast, scalar1=ROUND_MAGIC, scalar2=ROUND_MAGIC, op0=ALU.add, op1=ALU.subtract
            )

        def angles_2():
            fast = turns[:, :, :, 0:FAST]
            nc.vector.tensor_tensor(out=fast, in0=fast, in1=whole[:], op=ALU.subtract)

        def cos_and_sin():
            nc.scalar.activation(out=cos_sin[:], in_=turns[:], func=ACT.Sin, scale=2.0 * math.pi)

        spread = keep.tile([P, 2 * UV], BF16)

        def spread_rows(source, row, pair, second=BANK):
            copies = psum.tile([P, 2 * BANK], BF16, tag="bank")
            for i, width in enumerate((BANK, second)):
                nc.tensor.matmul(
                    copies[:, BANK * i : BANK * i + width],
                    lhsT=ident_bf16[:, row + i : row + i + 1].to_broadcast([P, P]),
                    rhs=source[:, 0:width],
                    start=True,
                    stop=True,
                )
            return pair, copies, BANK + second

        def keep_spread(engine_copy, pair, copies, width):
            engine_copy(out=spread[:, 2 * BANK * pair : 2 * BANK * pair + width], in_=copies[:, 0:width])

        x_codes = {}
        x_scales = {}

        def flip(t):
            flipped = psum.tile([P, PASSES, 2, P], F32, tag="bank")
            for g in range(PASSES):
                for u in range(2):
                    nc.tensor.transpose(
                        flipped[:, g, u, :], x_words[t][:, 256 * g + u : 256 * (g + 1) : 2], ident_f32[:]
                    )
            return flipped

        def group(flipped):
            grouped = stage.tile([P, PASSES, P, 4], BF16, align_bytes=64, tag="grouped")
            nc.scalar.copy(out=grouped[:].bitcast(F32), in_=flipped[:].rearrange("p g u r -> p g r u"))
            return grouped

        def quantise(t, grouped):
            x_codes[t] = keep.tile([P, PASSES * P], U32, align_bytes=64, name="x_codes_%d" % t)
            x_scales[t] = keep.tile([P, PASSES * P], U8, align_bytes=64, name="x_scales_%d" % t)
            nc.vector.quantize_mx(
                out=x_codes[t][:].bitcast(FP8X4),
                scales=x_scales[t][:],
                in_=grouped[:].rearrange("p g r j -> p (g r j)"),
            )

        def project(t, acc, first, width):
            chunk = max(c for c in w_words if W_EDGES[c] <= first)
            inside = first - W_EDGES[chunk]
            plane_first, plane = [(start, plane) for start, end, plane in scale_tiles if start <= first][-1]
            for g in range(PASSES):
                nc.tensor.matmul_mx(
                    out=acc,
                    lhsT=x_codes[t][:, P * g : P * (g + 1)].bitcast(FP8X4),
                    lhsT_scale=x_scales[t][:, P * g : P * (g + 1)],
                    rhs=w_words[chunk][:, g, 2 * inside : 2 * (inside + width)].bitcast(FP4X4),
                    rhs_scale=plane[:, g, first - plane_first : first - plane_first + width],
                    start=(g == 0),
                    stop=(g == PASSES - 1),
                )

        halves = keep.tile([P, 5, KEY], F32)

        def qk_front(first, count):
            acc_qk = psum.tile([P, count, KEY], F32, tag="bank")
            for i in range(count):
                project(first + i, acc_qk[:, i, :], 2 * UV, KEY)
            qk = qkpool.tile([P, count, KEY], F32, tag="qk")
            nc.vector.tensor_tensor(
                out=qk[:].rearrange("p t (h j) -> p t h j", h=2),
                in0=acc_qk[:].rearrange("p t (j h) -> p t h j", h=2),
                in1=halves[:, 0:1, :].to_broadcast([P, count, KEY]).rearrange("p t (h j) -> p t h j", h=2),
                op=ALU.add,
            )
            return first, count, qk

        def qk_back(first, count, qk):
            nc.scalar.activation(out=qk[:], in_=qk[:], func=ACT.Silu)
            scaled = qkpool.tile([P, count, 2, KEY], F32, tag="scaled")
            nc.gpsimd.tensor_tensor(
                out=scaled[:],
                in0=qk[:].unsqueeze(2).to_broadcast([P, count, 2, KEY]),
                in1=halves[:, 1:3, :].unsqueeze(1).to_broadcast([P, count, 2, KEY]),
                op=ALU.mult,
            )
            nc.gpsimd.tensor_tensor(
                out=scaled[:],
                in0=scaled[:],
                in1=halves[:, 3:5, :].unsqueeze(1).to_broadcast([P, count, 2, KEY]),
                op=ALU.add,
            )
            x1, x2 = scaled[:, :, :, 0:HALF], scaled[:, :, :, HALF:KEY]
            cos = cos_sin[:, 0, first : first + count, :].unsqueeze(2).to_broadcast([P, count, 2, HALF])
            sin = cos_sin[:, 1, first : first + count, :].unsqueeze(2).to_broadcast([P, count, 2, HALF])
            rotated = qkpool.tile([P, 2, count, KEY], F32, tag="rotated")
            by_token = rotated[:].rearrange("p c t f -> p t c f")
            for out, with_x1, with_x2, op in (
                (by_token[:, :, :, 0:HALF], cos, sin, ALU.subtract),
                (by_token[:, :, :, HALF:KEY], sin, cos, ALU.add),
            ):
                left = qkpool.tile([P, count, 2, HALF], F32, tag="left")
                right = qkpool.tile([P, count, 2, HALF], F32, tag="right")
                nc.gpsimd.tensor_tensor(out=left[:], in0=x1, in1=with_x1, op=ALU.mult)
                nc.gpsimd.tensor_tensor(out=right[:], in0=x2, in1=with_x2, op=ALU.mult)
                nc.gpsimd.tensor_tensor(out=out, in0=left[:], in1=right[:], op=op)
            return first, count, rotated

        def new_z(banks):
            z = zpool.tile([P, BANK * banks], F32, tag="z%d" % banks)
            return z

        def bank(z, b, t, half, column_bank):
            first = UV * half + BANK * column_bank
            acc = psum.tile([P, BANK], F32, tag="bank")
            project(t, acc[:], first, BANK)
            nc.vector.tensor_tensor(
                out=z[:, BANK * b : BANK * (b + 1)], in0=acc[:], in1=spread[:, first : first + BANK], op=ALU.add
            )

        def silu(z, b, count=1):
            part = z[:, BANK * b : BANK * (b + count)]
            nc.scalar.activation(out=part, in_=part, func=ACT.Silu)

        def store(z, t, half, column_bank, banks):
            nc.sync.dma_start(out=uv_dram[half][:, t, BANK * column_bank : BANK * (column_bank + banks)], in_=z[:])

        def silu_and_store(t, half, first_bank, banks, silu_banks=2, between=None):
            z = zpool.tile([P, BANK * banks], F32, tag="z%d" % banks)
            for b in range(banks):
                if between and b in between:
                    between[b]()
                first = UV * half + BANK * (first_bank + b)
                acc = psum.tile([P, BANK], F32, tag="bank")
                project(t, acc[:], first, BANK)
                nc.vector.tensor_tensor(
                    out=z[:, BANK * b : BANK * (b + 1)], in0=acc[:], in1=spread[:, first : first + BANK], op=ALU.add
                )
                if (b + 1) % silu_banks == 0 or b + 1 == banks:
                    done = BANK * (b - b % silu_banks)
                    nc.scalar.activation(
                        out=z[:, done : BANK * (b + 1)], in_=z[:, done : BANK * (b + 1)], func=ACT.Silu
                    )
            nc.sync.dma_start(
                out=uv_dram[half][:, t, BANK * first_bank : BANK * (first_bank + banks)], in_=z[:]
            )

        def store_q_and_k(batch):
            first, count, rotated = batch
            for c in range(2):
                nc.sync.dma_start(out=qk_dram[c][:, first : first + count, :], in_=rotated[:, c, :, :])

        banks_of_half = UV // BANK

        batches = {}
        ahead = {}

        def prepare(*tiles):
            flipped = [flip(t) for t in tiles]
            for t, f in zip(tiles, flipped):
                ahead[t] = group(f)

        def quantise_ahead(*tiles):
            for t in tiles:
                quantise(t, ahead[t])

        def batch(t):
            batches[t] = qk_back(*qk_front(t, 2))

        def spread_small():
            small = spread_rows(small_rows, 0, 4, KEY)[1]
            nc.vector.tensor_copy(
                out=halves[:].rearrange("p v (h j) -> p v h j", h=2),
                in_=small[:, 0 : 5 * KEY].rearrange("p (v j h) -> p v h j", v=5, h=2),
            )

        U, V4 = 0, 1
        flipped_0 = flip(0)
        grouped_0 = group(flipped_0)
        bias_01 = spread_rows(bias_rows, 0, 0)
        bias_23 = spread_rows(bias_rows, 2, 1)
        quantise(0, grouped_0)
        keep_spread(nc.vector.tensor_copy, *bias_01)
        keep_spread(nc.scalar.copy, *bias_23)
        later_loads()
        z = new_z(2)
        bank(z, 0, 0, 0, 0)
        bank(z, 1, 0, 0, 1)
        silu(z, 0)
        release_angles()
        prepare(1)
        bias_45 = spread_rows(bias_rows, 4, 2)
        bias_67 = spread_rows(bias_rows, 6, 3)
        silu(z, 1)
        store(z, 0, 0, 0, 2)
        keep_spread(nc.scalar.copy, *bias_45)
        keep_spread(nc.scalar.copy, *bias_67)
        z = new_z(2)
        quantise_ahead(1)
        bank(z, 0, 0, 0, 2)
        angles_2()
        bank(z, 1, 0, 0, 3)
        silu(z, 0)
        silu(z, 1)
        store(z, 0, 0, 2, 2)
        cos_and_sin()
        silu_and_store(1, 0, 0, 4)
        prepare(2, 3)
        spread_small()
        front = qk_front(0, 2)
        batches[0] = qk_back(*front)
        silu_and_store(0, V4, 0, 4, 2, {2: lambda: quantise_ahead(2, 3)})
        silu_and_store(1, V4, 0, 4)
        prepare(4, 5)
        silu_and_store(2, U, 0, 4)
        silu_and_store(3, U, 0, 4, 2, {2: lambda: (quantise_ahead(4, 5), batch(2))})
        silu_and_store(2, V4, 0, 4)
        store_q_and_k(batches[0])
        prepare(6, 7)
        silu_and_store(3, V4, 0, 4)
        silu_and_store(4, U, 0, 4)
        quantise_ahead(6, 7)
        batch(4)
        silu_and_store(5, U, 0, 4)
        store_q_and_k(batches[2])
        silu_and_store(4, V4, 0, 4)
        batch(6)
        silu_and_store(5, V4, 0, 4)
        silu_and_store(6, U, 0, 4)
        store_q_and_k(batches[4])
        silu_and_store(7, U, 0, 4)
        silu_and_store(6, V4, 0, 4)
        silu_and_store(7, V4, 0, 2)
        store_q_and_k(batches[6])
        silu_and_store(7, V4, 2, 2)
